import numpy as np
import ml_dtypes


def mxq(x, axis, fmt="e4m3"):
    dtype, down = {"e4m3": (ml_dtypes.float8_e4m3fn, 7), "e5m2": (ml_dtypes.float8_e5m2, 14)}[fmt]
    v = np.moveaxis(np.asarray(x, np.float32).astype(ml_dtypes.bfloat16).astype(np.float64), axis, -1)
    blocks = v.reshape(v.shape[:-1] + (-1, 32))
    amax = np.abs(blocks).max(-1, keepdims=True)
    byte = np.maximum(np.where(amax > 0, np.frexp(amax)[1] - 1 + 127, 0) - down, 1)
    scale = np.exp2(byte - 127.0)
    codes = (blocks / scale).astype(np.float32).astype(dtype).astype(np.float64)
    return np.moveaxis((codes * scale).reshape(v.shape), -1, axis)


WIDE = False


def mx_kscale(k):
    if not WIDE:
        return np.ones(k)
    levels = np.array([10, -10, 5, -5, 0])
    if k % 512:
        return np.exp2(np.random.permutation(np.resize(levels, k // 32))).repeat(32)
    a = np.empty((k // 512, 16))
    for p in range(k // 512):
        a[p, :8] = np.random.permutation(np.resize(levels, 8))
        for g in range(8):
            far = levels[np.abs(levels - a[p, g]) >= 10]
            a[p, g + 8] = far[np.random.randint(len(far))]
    return np.exp2(a.ravel()).repeat(32)


BF16 = ml_dtypes.bfloat16


def bf(x):
    return np.asarray(x, np.float32).astype(BF16)


def f64(x):
    return np.asarray(x).astype(np.float64)


B, NH, T, D, N, CK = 1, 6, 1024, 512, 256, 512
KD = NH * N
EPS_LN = 1e-5
TARGET_ACTIVITY = 0.1


def layernorm(v):
    m = np.mean(v, axis=-1, keepdims=True)
    var = np.mean((v - m) ** 2, axis=-1, keepdims=True)
    return (v - m) / np.sqrt(var + EPS_LN)


def setup_inputs():
    t = mx_kscale(KD)
    xy = np.maximum(np.random.standard_normal((B, NH, T, N)) * 0.5, 0.0) * np.maximum(np.random.standard_normal((B, NH, T, N)), 0.0)
    return {'xy_sparse': bf(xy * t.reshape(NH, 1, N)),
            'decoder': bf(np.random.standard_normal((KD, D)) * 2.0 / np.sqrt(KD) / t[:, None]),
            'x': bf(np.random.standard_normal((B, 1, T, D))),
            'scale': bf(1.0 + 0.1 * np.random.standard_normal(D)),
            'running_activity': bf(TARGET_ACTIVITY * np.exp(0.5 * np.random.standard_normal(D)))}


def reference(xy_sparse, decoder, x, scale, running_activity):
    flat = f64(xy_sparse).transpose(0, 2, 1, 3).reshape(B, 1, T, KD)
    y_mlp = mxq(flat, 3, 'e4m3') @ mxq(f64(decoder), 0, 'e4m3')
    y = layernorm(y_mlp)
    regulation = TARGET_ACTIVITY / (f64(running_activity) + 1e-6)
    y = y * np.sqrt(regulation) * f64(scale)
    return layernorm(f64(x) + y)

@@ -1,0 +1,318 @@
+from contextlib import ExitStack
+
+import concourse.mybir as mybir
+from concourse.masks import make_identity
+
+F32 = mybir.dt.float32
+BF16 = mybir.dt.bfloat16
+U32 = mybir.dt.uint32
+U8 = mybir.dt.uint8
+FP8X4 = mybir.dt.float8_e4m3fn_x4
+ALU = mybir.AluOpType
+ACT = mybir.ActivationFunctionType
+
+P = 128
+PACK = 4
+K_PASS = P * PACK
+
+HEADS = 6
+TOKENS = 1024
+FEATS = 256
+D = 512
+PASSES = HEADS * FEATS // K_PASS
+HEADS_PER_PASS = K_PASS // FEATS
+WORDS = FEATS // 2
+TILES = TOKENS // P
+PAIR = 2
+PAIRS = TILES // PAIR
+GAIN_ROWS = D // P
+RUN = 4
+DEC_COLS_VECTOR = (2 * D // 3) // RUN * RUN
+
+EPS_LN = 1e-5
+EPS_ACTIVITY = 1e-6
+TARGET_ACTIVITY = 0.1
+
+FLOPS = 2 * TOKENS * HEADS * FEATS * D
+
+
+def tile_bdhlayer_pc_kernel(tc, xy_sparse, decoder, x, scale, running_activity, out):
+    nc = tc.nc
+
+    xy_view = xy_sparse[0].rearrange("h (p n) f -> p h n f", n=TILES)
+    x_view = x[0, 0].rearrange("(p n) d -> p n d", n=TILES)
+    out_view = out[0, 0].rearrange("(p n) d -> p n d", n=TILES)
+    dec_view = decoder.rearrange("(g q t) d -> q g (t d)", g=PASSES, t=PACK)
+
+    with ExitStack() as ctx:
+        const = ctx.enter_context(tc.tile_pool(name="const", bufs=1))
+        loads = ctx.enter_context(tc.tile_pool(name="loads", bufs=PAIRS))
+        work = ctx.enter_context(tc.tile_pool(name="work", bufs=3))
+        small = ctx.enter_context(tc.tile_pool(name="small", bufs=4))
+        psum_t = ctx.enter_context(tc.psum_pool(name="psum_t", bufs=2 * PASSES))
+        psum_y = ctx.enter_context(tc.psum_pool(name="psum_y", bufs=2))
+        ctx.enter_context(tc.manual_schedule())
+
+        ident = const.tile([P, P], F32)
+        make_identity(nc, ident[:])
+        eps_ln = const.tile([P, 1], F32)
+        nc.vector.memset(eps_ln[:], EPS_LN)
+        eps_activity = const.tile([P, 1], F32)
+        nc.vector.memset(eps_activity[:], EPS_ACTIVITY / TARGET_ACTIVITY)
+        vectors = const.tile([P, 2, P], BF16)
+        nc.vector.memset(vectors[:], 1.0)
+
+        dec_raw = const.tile([P, PASSES, PACK, D], BF16)
+
+        def load_decoder(g):
+            nc.sync.dma_start(
+                out=dec_raw[:, g].rearrange("p t d -> p (t d)"),
+                in_=dec_view[:, g],
+            )
+
+        load_decoder(0)
+        nc.sync.dma_start(
+            out=vectors[0:GAIN_ROWS, 0, :],
+            in_=running_activity.rearrange("(j c) -> j c", j=GAIN_ROWS),
+        )
+        nc.sync.dma_start(
+            out=vectors[0:GAIN_ROWS, 1, :], in_=scale.rearrange("(j c) -> j c", j=GAIN_ROWS)
+        )
+        for g in range(1, PASSES):
+            load_decoder(g)
+
+        xy_tiles = []
+        x_tiles = []
+
+        def load_xy(j):
+            xy_sb = loads.tile([P, PAIR, HEADS, FEATS], BF16, name="xy_sb")
+            for i in range(PAIR):
+                nc.sync.dma_start(out=xy_sb[:, i], in_=xy_view[:, :, PAIR * j + i, :])
+            xy_tiles.append(xy_sb)
+
+        def load_x(j):
+            x_sb = loads.tile([P, PAIR, D], BF16, name="x_sb")
+            nc.sync.dma_start(out=x_sb[:], in_=x_view[:, PAIR * j : PAIR * (j + 1), :])
+            x_tiles.append(x_sb)
+
+        load_xy(0)
+        for j in range(PAIRS):
+            if j + 1 < PAIRS:
+                load_xy(j + 1)
+            load_x(j)
+
+        regulation = const.tile([P, P], F32)
+        nc.scalar.activation(
+            out=regulation[:],
+            in_=vectors[:, 0, :],
+            func=ACT.Abs_reciprocal_sqrt,
+            scale=1.0 / TARGET_ACTIVITY,
+            bias=eps_activity[:],
+        )
+        gain_rows = const.tile([P, P], F32)
+        nc.vector.tensor_tensor(
+            out=gain_rows[:], in0=regulation[:], in1=vectors[:, 1, :], op=ALU.mult
+        )
+        gain_ps = psum_y.tile([P, D], F32, name="acc")
+        for j in range(GAIN_ROWS):
+            nc.tensor.matmul(
+                out=gain_ps[:, P * j : P * (j + 1)],
+                lhsT=ident[:, j : j + 1].to_broadcast([P, P]),
+                rhs=gain_rows[:],
+                start=True,
+                stop=True,
+            )
+        gain = const.tile([P, D], F32)
+
+        dec_grouped = const.tile([P, PASSES, D, PACK], BF16, align_bytes=64)
+        dec_codes = const.tile([P, PASSES, D], U32, align_bytes=64)
+        dec_scales = const.tile([P, PASSES, D], U8, align_bytes=64)
+
+        def regroup_decoder(g):
+            nc.vector.tensor_copy(
+                out=dec_grouped[:, g, :DEC_COLS_VECTOR, :].rearrange("p (c i) t -> p c t i", i=RUN),
+                in_=dec_raw[:, g, :, :DEC_COLS_VECTOR].rearrange("p t (c i) -> p c t i", i=RUN),
+            )
+            nc.scalar.copy(
+                out=dec_grouped[:, g, DEC_COLS_VECTOR:, :].rearrange("p (c i) t -> p c t i", i=RUN),
+                in_=dec_raw[:, g, :, DEC_COLS_VECTOR:].rearrange("p t (c i) -> p c t i", i=RUN),
+            )
+
+        def quantise_decoder(g):
+            nc.vector.quantize_mx(
+                out=dec_codes[:, g, :].bitcast(FP8X4),
+                scales=dec_scales[:, g, :],
+                in_=dec_grouped[:, g].rearrange("p d t -> p (d t)"),
+            )
+
+        regroup_decoder(0)
+        nc.scalar.copy(out=gain[:], in_=gain_ps[:])
+        for g in range(1, PASSES):
+            regroup_decoder(g)
+            quantise_decoder(g - 1)
+        quantise_decoder(PASSES - 1)
+
+        banks = {}
+        grouped = {}
+        codes = {}
+        acc = {}
+        stat = {}
+        centred = {}
+        z = {}
+
+        def transpose_pair(j):
+            xy_words = xy_tiles[j][:].rearrange("p n h f -> p n (h f)").bitcast(F32)
+            banks[j] = [
+                psum_t.tile([P, PAIR, HEADS_PER_PASS, P], F32, name="bank") for g in range(PASSES)
+            ]
+            for i in range(PAIR):
+                for g in range(PASSES):
+                    for u in range(HEADS_PER_PASS):
+                        nc.tensor.transpose(
+                            banks[j][g][:, i, u, :],
+                            xy_words[:, i, 2 * P * g + u : 2 * P * (g + 1) : 2],
+                            ident[:],
+                        )
+
+        def evacuate_tile(t):
+            grouped[t] = work.tile([P, PASSES, P, PACK], BF16, align_bytes=64, name="xy_grouped")
+            for g in range(PASSES):
+                nc.scalar.copy(
+                    out=grouped[t][:, g].bitcast(F32),
+                    in_=banks[t // PAIR][g][:, t % PAIR].rearrange("p u r -> p r u"),
+                )
+
+        def quantise_tile(t):
+            xy_codes = work.tile([P, PASSES, P], U32, align_bytes=64, name="xy_codes")
+            xy_scales = work.tile([P, PASSES, P], U8, align_bytes=64, name="xy_scales")
+            for g in range(PASSES):
+                nc.vector.quantize_mx(
+                    out=xy_codes[:, g, :].bitcast(FP8X4),
+                    scales=xy_scales[:, g, :],
+                    in_=grouped[t][:, g].rearrange("p r t -> p (r t)"),
+                )
+            codes[t] = (xy_codes, xy_scales)
+
+        def multiply(t):
+            xy_codes, xy_scales = codes[t]
+            acc[t] = psum_y.tile([P, D], F32, name="acc")
+            for g in range(PASSES):
+                nc.tensor.matmul_mx(
+                    out=acc[t][:],
+                    lhsT=xy_codes[:, g, :].bitcast(FP8X4),
+                    lhsT_scale=xy_scales[:, g, :],
+                    rhs=dec_codes[:, g, :].bitcast(FP8X4),
+                    rhs_scale=dec_scales[:, g, :],
+                    start=(g == 0),
+                    stop=(g == PASSES - 1),
+                )
+
+        def new_stat(name, t, width):
+            stat[(name, t)] = small.tile([P, width], F32, name=name)
+            return stat[(name, t)]
+
+        def first_stats(t):
+            nc.vector.bn_stats(out=new_stat("partial", t, 6)[:], in_=acc[t][:])
+
+        def first_mean_var(t):
+            nc.vector.bn_aggr(out=new_stat("mean_var", t, 2)[:], in_=stat[("partial", t)][:])
+
+        def first_rstd(t):
+            nc.scalar.activation(
+                out=new_stat("rstd1", t, 1)[:],
+                in_=stat[("mean_var", t)][:, 1:2],
+                func=ACT.Abs_reciprocal_sqrt,
+                bias=eps_ln[:],
+            )
+
+        def centre_and_gain(t):
+            centred[t] = work.tile([P, D], F32, name="centred")
+            nc.vector.scalar_tensor_tensor(
+                out=centred[t][:],
+                in0=acc[t][:],
+                scalar=stat[("mean_var", t)][:, 0:1],
+                in1=gain[:],
+                op0=ALU.subtract,
+                op1=ALU.mult,
+            )
+
+        def add_residual(t):
+            z[t] = work.tile([P, D], F32, name="z")
+            nc.vector.scalar_tensor_tensor(
+                out=z[t][:],
+                in0=centred[t][:],
+                scalar=stat[("rstd1", t)][:],
+                in1=x_tiles[t // PAIR][:, t % PAIR, :],
+                op0=ALU.mult,
+                op1=ALU.add,
+                accum_out=new_stat("z_sum", t, 1)[:],
+            )
+
+        def second_sum_of_squares(t):
+            squares = work.tile([P, D], F32, name="squares")
+            nc.scalar.activation(
+                out=squares[:],
+                in_=z[t][:],
+                func=ACT.Square,
+                scale=-float(D),
+                bias=stat[("z_sum", t)][:],
+                accum_out=new_stat("sum_sq", t, 1)[:],
+            )
+
+        def second_rstd(t):
+            nc.scalar.activation(
+                out=new_stat("rstd2", t, 1)[:],
+                in_=stat[("sum_sq", t)][:],
+                func=ACT.Abs_reciprocal_sqrt,
+                scale=1.0 / float(D * D * D),
+                bias=eps_ln[:],
+            )
+
+        def second_shift(t):
+            nc.gpsimd.tensor_scalar(
+                out=new_stat("shift2", t, 1)[:],
+                in0=stat[("z_sum", t)][:],
+                scalar1=stat[("rstd2", t)][:],
+                scalar2=-1.0 / float(D),
+                op0=ALU.mult,
+                op1=ALU.mult,
+            )
+
+        def normalise_and_store(t):
+            result = work.tile([P, D], F32, name="result")
+            nc.scalar.activation(
+                out=result[:],
+                in_=z[t][:],
+                func=ACT.Identity,
+                scale=stat[("rstd2", t)][:],
+                bias=stat[("shift2", t)][:],
+            )
+            nc.sync.dma_start(out=out_view[:, t, :], in_=result[:])
+
+        def live(t):
+            return 0 <= t < TILES
+
+        for t in range(-3, TILES + 2):
+            if live(t):
+                first_stats(t)
+            if live(t + 1):
+                quantise_tile(t + 1)
+                multiply(t + 1)
+            if live(t + 3) and (t + 3) % PAIR == 0:
+                transpose_pair((t + 3) // PAIR)
+            if live(t):
+                first_mean_var(t)
+            if live(t - 2):
+                second_rstd(t - 2)
+                second_shift(t - 2)
+            if live(t + 2):
+                evacuate_tile(t + 2)
+            if live(t):
+                first_rstd(t)
+            if live(t - 2):
+                normalise_and_store(t - 2)
+            if live(t - 1):
+                add_residual(t - 1)
+                second_sum_of_squares(t - 1)
+            if live(t):
+                centre_and_gain(t)

@@ -27,7 +27,7 @@ PAIR = 2
 PAIRS = TILES // PAIR
 GAIN_ROWS = D // P
 RUN = 4
-DEC_COLS_VECTOR = (2 * D // 3) // RUN * RUN
+DEC_COLS_VECTOR = 5 * D // 8
 
 EPS_LN = 1e-5
 EPS_ACTIVITY = 1e-6
@@ -42,7 +42,7 @@ def tile_bdhlayer_pc_kernel(tc, xy_sparse, decoder, x, scale, running_activity, 
     xy_view = xy_sparse[0].rearrange("h (p n) f -> p h n f", n=TILES)
     x_view = x[0, 0].rearrange("(p n) d -> p n d", n=TILES)
     out_view = out[0, 0].rearrange("(p n) d -> p n d", n=TILES)
-    dec_view = decoder.rearrange("(g q t) d -> q g (t d)", g=PASSES, t=PACK)
+    dec_view = decoder.rearrange("(g q t) d -> q g t d", g=PASSES, t=PACK)
 
     with ExitStack() as ctx:
         const = ctx.enter_context(tc.tile_pool(name="const", bufs=1))
@@ -53,33 +53,29 @@ def tile_bdhlayer_pc_kernel(tc, xy_sparse, decoder, x, scale, running_activity, 
         psum_y = ctx.enter_context(tc.psum_pool(name="psum_y", bufs=2))
         ctx.enter_context(tc.manual_schedule())
 
-        ident = const.tile([P, P], F32)
-        make_identity(nc, ident[:])
         eps_ln = const.tile([P, 1], F32)
         nc.vector.memset(eps_ln[:], EPS_LN)
         eps_activity = const.tile([P, 1], F32)
         nc.vector.memset(eps_activity[:], EPS_ACTIVITY / TARGET_ACTIVITY)
-        vectors = const.tile([P, 2, P], BF16)
-        nc.vector.memset(vectors[:], 1.0)
-
+        gain_rows = const.tile([P, P], F32)
+        nc.vector.memset(gain_rows[:], 0.0)
+        ident = const.tile([P, P], F32)
+        make_identity(nc, ident[:])
+        vectors = const.tile([GAIN_ROWS, 2, P], BF16)
         dec_raw = const.tile([P, PASSES, PACK, D], BF16)
 
-        def load_decoder(g):
-            nc.sync.dma_start(
-                out=dec_raw[:, g].rearrange("p t d -> p (t d)"),
-                in_=dec_view[:, g],
-            )
-
-        load_decoder(0)
-        nc.sync.dma_start(
-            out=vectors[0:GAIN_ROWS, 0, :],
-            in_=running_activity.rearrange("(j c) -> j c", j=GAIN_ROWS),
+        nc.scalar.dma_start(
+            out=vectors[:, 0, :], in_=running_activity.rearrange("(j c) -> j c", j=GAIN_ROWS)
         )
-        nc.sync.dma_start(
-            out=vectors[0:GAIN_ROWS, 1, :], in_=scale.rearrange("(j c) -> j c", j=GAIN_ROWS)
+        nc.scalar.dma_start(
+            out=vectors[:, 1, :], in_=scale.rearrange("(j c) -> j c", j=GAIN_ROWS)
         )
+        warm_up = const.tile([P, 1], F32)
+        nc.scalar.activation(out=warm_up[:], in_=eps_ln[:], func=ACT.Abs_reciprocal_sqrt)
+        for cols in (slice(0, DEC_COLS_VECTOR), slice(DEC_COLS_VECTOR, D)):
+            nc.sync.dma_start(out=dec_raw[:, 0, :, cols], in_=dec_view[:, 0, :, cols])
         for g in range(1, PASSES):
-            load_decoder(g)
+            nc.sync.dma_start(out=dec_raw[:, g], in_=dec_view[:, g])
 
         xy_tiles = []
         x_tiles = []
@@ -101,28 +97,29 @@ def tile_bdhlayer_pc_kernel(tc, xy_sparse, decoder, x, scale, running_activity, 
                 load_xy(j + 1)
             load_x(j)
 
-        regulation = const.tile([P, P], F32)
+        regulation = const.tile([GAIN_ROWS, P], F32)
         nc.scalar.activation(
             out=regulation[:],
             in_=vectors[:, 0, :],
             func=ACT.Abs_reciprocal_sqrt,
             scale=1.0 / TARGET_ACTIVITY,
-            bias=eps_activity[:],
-        )
-        gain_rows = const.tile([P, P], F32)
-        nc.vector.tensor_tensor(
-            out=gain_rows[:], in0=regulation[:], in1=vectors[:, 1, :], op=ALU.mult
+            bias=eps_activity[0:GAIN_ROWS, :],
         )
         gain_ps = psum_y.tile([P, D], F32, name="acc")
-        for j in range(GAIN_ROWS):
-            nc.tensor.matmul(
-                out=gain_ps[:, P * j : P * (j + 1)],
-                lhsT=ident[:, j : j + 1].to_broadcast([P, P]),
-                rhs=gain_rows[:],
-                start=True,
-                stop=True,
-            )
         gain = const.tile([P, D], F32)
+
+        def spread_gain():
+            nc.vector.tensor_tensor(
+                out=gain_rows[0:GAIN_ROWS, :], in0=regulation[:], in1=vectors[:, 1, :], op=ALU.mult
+            )
+            for j in range(GAIN_ROWS):
+                nc.tensor.matmul(
+                    out=gain_ps[:, P * j : P * (j + 1)],
+                    lhsT=ident[:, j : j + 1].to_broadcast([P, P]),
+                    rhs=gain_rows[:],
+                    start=True,
+                    stop=True,
+                )
 
         dec_grouped = const.tile([P, PASSES, D, PACK], BF16, align_bytes=64)
         dec_codes = const.tile([P, PASSES, D], U32, align_bytes=64)
@@ -146,10 +143,11 @@ def tile_bdhlayer_pc_kernel(tc, xy_sparse, decoder, x, scale, running_activity, 
             )
 
         regroup_decoder(0)
-        nc.scalar.copy(out=gain[:], in_=gain_ps[:])
+        spread_gain()
         for g in range(1, PASSES):
             regroup_decoder(g)
             quantise_decoder(g - 1)
+        nc.scalar.copy(out=gain[:], in_=gain_ps[:])
         quantise_decoder(PASSES - 1)
 
         banks = {}

@@ -49,8 +49,8 @@ def tile_bdhlayer_pc_kernel(tc, xy_sparse, decoder, x, scale, running_activity, 
         loads = ctx.enter_context(tc.tile_pool(name="loads", bufs=PAIRS))
         work = ctx.enter_context(tc.tile_pool(name="work", bufs=3))
         small = ctx.enter_context(tc.tile_pool(name="small", bufs=4))
-        psum_t = ctx.enter_context(tc.psum_pool(name="psum_t", bufs=2 * PASSES))
-        psum_y = ctx.enter_context(tc.psum_pool(name="psum_y", bufs=2))
+        psum_t = ctx.enter_context(tc.psum_pool(name="psum_t", bufs=3))
+        psum_y = ctx.enter_context(tc.psum_pool(name="psum_y", bufs=3))
         ctx.enter_context(tc.manual_schedule())
 
         eps_ln = const.tile([P, 1], F32)
@@ -72,18 +72,12 @@ def tile_bdhlayer_pc_kernel(tc, xy_sparse, decoder, x, scale, running_activity, 
         )
         warm_up = const.tile([P, 1], F32)
         nc.scalar.activation(out=warm_up[:], in_=eps_ln[:], func=ACT.Abs_reciprocal_sqrt)
-        for cols in (slice(0, DEC_COLS_VECTOR), slice(DEC_COLS_VECTOR, D)):
-            nc.sync.dma_start(out=dec_raw[:, 0, :, cols], in_=dec_view[:, 0, :, cols])
-        for g in range(1, PASSES):
-            nc.sync.dma_start(out=dec_raw[:, g], in_=dec_view[:, g])
-
         xy_tiles = []
         x_tiles = []
 
-        def load_xy(j):
-            xy_sb = loads.tile([P, PAIR, HEADS, FEATS], BF16, name="xy_sb")
-            for i in range(PAIR):
-                nc.sync.dma_start(out=xy_sb[:, i], in_=xy_view[:, :, PAIR * j + i, :])
+        def load_xy(t):
+            xy_sb = loads.tile([P, HEADS, FEATS], BF16, name="xy_sb", bufs=TILES)
+            nc.sync.dma_start(out=xy_sb[:], in_=xy_view[:, :, t, :])
             xy_tiles.append(xy_sb)
 
         def load_x(j):
@@ -91,11 +85,15 @@ def tile_bdhlayer_pc_kernel(tc, xy_sparse, decoder, x, scale, running_activity, 
             nc.sync.dma_start(out=x_sb[:], in_=x_view[:, PAIR * j : PAIR * (j + 1), :])
             x_tiles.append(x_sb)
 
+        for cols in (slice(0, DEC_COLS_VECTOR), slice(DEC_COLS_VECTOR, D)):
+            nc.sync.dma_start(out=dec_raw[:, 0, :, cols], in_=dec_view[:, 0, :, cols])
         load_xy(0)
-        for j in range(PAIRS):
-            if j + 1 < PAIRS:
-                load_xy(j + 1)
-            load_x(j)
+        for g in range(1, PASSES):
+            nc.sync.dma_start(out=dec_raw[:, g], in_=dec_view[:, g])
+        for t in range(1, TILES):
+            load_xy(t)
+            if t % PAIR == 1:
+                load_x(t // PAIR)
 
         regulation = const.tile([GAIN_ROWS, P], F32)
         nc.scalar.activation(
@@ -142,14 +140,6 @@ def tile_bdhlayer_pc_kernel(tc, xy_sparse, decoder, x, scale, running_activity, 
                 in_=dec_grouped[:, g].rearrange("p d t -> p (d t)"),
             )
 
-        regroup_decoder(0)
-        spread_gain()
-        for g in range(1, PASSES):
-            regroup_decoder(g)
-            quantise_decoder(g - 1)
-        nc.scalar.copy(out=gain[:], in_=gain_ps[:])
-        quantise_decoder(PASSES - 1)
-
         banks = {}
         grouped = {}
         codes = {}
@@ -158,36 +148,36 @@ def tile_bdhlayer_pc_kernel(tc, xy_sparse, decoder, x, scale, running_activity, 
         centred = {}
         z = {}
 
-        def transpose_pair(j):
-            xy_words = xy_tiles[j][:].rearrange("p n h f -> p n (h f)").bitcast(F32)
-            banks[j] = [
-                psum_t.tile([P, PAIR, HEADS_PER_PASS, P], F32, name="bank") for g in range(PASSES)
+        def transpose_tile(t):
+            words = xy_tiles[t][:].rearrange("p h f -> p (h f)").bitcast(F32)
+            banks[t] = [
+                psum_t.tile([P, 2, 2, P], F32, name="bank_a"),
+                psum_t.tile([P, 1, 2, P], F32, name="bank_b", bufs=2),
             ]
-            for i in range(PAIR):
-                for g in range(PASSES):
-                    for u in range(HEADS_PER_PASS):
-                        nc.tensor.transpose(
-                            banks[j][g][:, i, u, :],
-                            xy_words[:, i, 2 * P * g + u : 2 * P * (g + 1) : 2],
-                            ident[:],
-                        )
+            for g in range(PASSES):
+                for u in range(2):
+                    nc.tensor.transpose(
+                        banks[t][g // 2][:, g % 2, u, :],
+                        words[:, 2 * P * g + u : 2 * P * (g + 1) : 2],
+                        ident[:],
+                    )
 
         def evacuate_tile(t):
             grouped[t] = work.tile([P, PASSES, P, PACK], BF16, align_bytes=64, name="xy_grouped")
-            for g in range(PASSES):
+            for b, passes in enumerate((slice(0, 2), slice(2, 3))):
                 nc.scalar.copy(
-                    out=grouped[t][:, g].bitcast(F32),
-                    in_=banks[t // PAIR][g][:, t % PAIR].rearrange("p u r -> p r u"),
+                    out=grouped[t][:, passes].bitcast(F32),
+                    in_=banks[t][b][:].rearrange("p g u r -> p g r u"),
                 )
 
         def quantise_tile(t):
             xy_codes = work.tile([P, PASSES, P], U32, align_bytes=64, name="xy_codes")
             xy_scales = work.tile([P, PASSES, P], U8, align_bytes=64, name="xy_scales")
-            for g in range(PASSES):
+            for passes in (slice(0, 2), slice(2, 3)):
                 nc.vector.quantize_mx(
-                    out=xy_codes[:, g, :].bitcast(FP8X4),
-                    scales=xy_scales[:, g, :],
-                    in_=grouped[t][:, g].rearrange("p r t -> p (r t)"),
+                    out=xy_codes[:, passes, :].rearrange("p g r -> p (g r)").bitcast(FP8X4),
+                    scales=xy_scales[:, passes, :].rearrange("p g r -> p (g r)"),
+                    in_=grouped[t][:, passes].rearrange("p g r t -> p (g r t)"),
                 )
             codes[t] = (xy_codes, xy_scales)
 
@@ -267,7 +257,7 @@ def tile_bdhlayer_pc_kernel(tc, xy_sparse, decoder, x, scale, running_activity, 
             )
 
         def second_shift(t):
-            nc.gpsimd.tensor_scalar(
+            nc.vector.tensor_scalar(
                 out=new_stat("shift2", t, 1)[:],
                 in0=stat[("z_sum", t)][:],
                 scalar1=stat[("rstd2", t)][:],
@@ -276,41 +266,67 @@ def tile_bdhlayer_pc_kernel(tc, xy_sparse, decoder, x, scale, running_activity, 
                 op1=ALU.mult,
             )
 
-        def normalise_and_store(t):
+        def normalise_and_store(t, engine):
             result = work.tile([P, D], F32, name="result")
-            nc.scalar.activation(
+            engine.tensor_scalar(
                 out=result[:],
-                in_=z[t][:],
-                func=ACT.Identity,
-                scale=stat[("rstd2", t)][:],
-                bias=stat[("shift2", t)][:],
+                in0=z[t][:],
+                scalar1=stat[("rstd2", t)][:],
+                scalar2=stat[("shift2", t)][:],
+                op0=ALU.mult,
+                op1=ALU.add,
             )
             nc.sync.dma_start(out=out_view[:, t, :], in_=result[:])
 
         def live(t):
             return 0 <= t < TILES
 
-        for t in range(-3, TILES + 2):
-            if live(t):
-                first_stats(t)
-            if live(t + 1):
-                quantise_tile(t + 1)
-                multiply(t + 1)
-            if live(t + 3) and (t + 3) % PAIR == 0:
-                transpose_pair((t + 3) // PAIR)
-            if live(t):
-                first_mean_var(t)
-            if live(t - 2):
-                second_rstd(t - 2)
-                second_shift(t - 2)
+        regroup_decoder(0)
+        transpose_tile(0)
+        spread_gain()
+        evacuate_tile(0)
+        quantise_decoder(0)
+        regroup_decoder(1)
+        transpose_tile(1)
+        quantise_tile(0)
+        regroup_decoder(2)
+        quantise_decoder(1)
+        evacuate_tile(1)
+        quantise_decoder(2)
+        nc.scalar.copy(out=gain[:], in_=gain_ps[:])
+        multiply(0)
+        transpose_tile(2)
+        quantise_tile(1)
+        evacuate_tile(2)
+        multiply(1)
+        transpose_tile(3)
+        first_stats(0)
+        quantise_tile(2)
+        first_mean_var(0)
+        first_rstd(0)
+        evacuate_tile(3)
+        transpose_tile(4)
+        for t in range(TILES):
             if live(t + 2):
-                evacuate_tile(t + 2)
-            if live(t):
-                first_rstd(t)
+                multiply(t + 2)
             if live(t - 2):
-                normalise_and_store(t - 2)
-            if live(t - 1):
-                add_residual(t - 1)
-                second_sum_of_squares(t - 1)
-            if live(t):
-                centre_and_gain(t)
+                second_shift(t - 2)
+                normalise_and_store(t - 2, nc.gpsimd)
+            if live(t + 1):
+                first_stats(t + 1)
+            centre_and_gain(t)
+            if live(t + 4):
+                evacuate_tile(t + 4)
+            if live(t + 1):
+                first_mean_var(t + 1)
+                first_rstd(t + 1)
+            if live(t + 3):
+                quantise_tile(t + 3)
+            if live(t + 5):
+                transpose_tile(t + 5)
+            add_residual(t)
+            second_sum_of_squares(t)
+            second_rstd(t)
+        for t in (TILES - 2, TILES - 1):
+            second_shift(t)
+            normalise_and_store(t, nc.vector)

@@ -29,6 +29,8 @@ GAIN_ROWS = D // P
 RUN = 4
 DEC_COLS_VECTOR = 5 * D // 8
 
+SCALAR_STATS = ()
+
 EPS_LN = 1e-5
 EPS_ACTIVITY = 1e-6
 TARGET_ACTIVITY = 0.1
@@ -92,8 +94,9 @@ def tile_bdhlayer_pc_kernel(tc, xy_sparse, decoder, x, scale, running_activity, 
             nc.sync.dma_start(out=dec_raw[:, g], in_=dec_view[:, g])
         for t in range(1, TILES):
             load_xy(t)
-            if t % PAIR == 1:
-                load_x(t // PAIR)
+            if t >= 3 and t % PAIR == 1:
+                load_x(t // PAIR - 1)
+        load_x(PAIRS - 1)
 
         regulation = const.tile([GAIN_ROWS, P], F32)
         nc.scalar.activation(
@@ -203,7 +206,9 @@ def tile_bdhlayer_pc_kernel(tc, xy_sparse, decoder, x, scale, running_activity, 
             nc.vector.bn_stats(out=new_stat("partial", t, 6)[:], in_=acc[t][:])
 
         def first_mean_var(t):
-            nc.vector.bn_aggr(out=new_stat("mean_var", t, 2)[:], in_=stat[("partial", t)][:])
+            mean_var = new_stat("mean_var", t, 2)
+            nc.vector.bn_aggr(out=mean_var[:], in_=stat[("partial", t)][:])
+            stat[("mean1", t)] = mean_var[:, 0:1]
 
         def first_rstd(t):
             nc.scalar.activation(
@@ -213,12 +218,40 @@ def tile_bdhlayer_pc_kernel(tc, xy_sparse, decoder, x, scale, running_activity, 
                 bias=eps_ln[:],
             )
 
+        def first_sum(t):
+            passed = work.tile([P, D], F32, name="passed")
+            nc.scalar.activation(
+                out=passed[:], in_=acc[t][:], func=ACT.Identity, accum_out=new_stat("y_sum", t, 1)[:]
+            )
+
+        def first_sum_of_squares(t):
+            passed = work.tile([P, D], F32, name="passed")
+            nc.scalar.activation(
+                out=passed[:],
+                in_=acc[t][:],
+                func=ACT.Square,
+                scale=-float(D),
+                bias=stat[("y_sum", t)][:],
+                accum_out=new_stat("y_sum_sq", t, 1)[:],
+            )
+            stat[("mean1", t)] = new_stat("y_mean", t, 1)[:]
+            nc.scalar.activation(
+                out=stat[("mean1", t)], in_=stat[("y_sum", t)][:], func=ACT.Copy, scale=1.0 / float(D)
+            )
+            nc.scalar.activation(
+                out=new_stat("rstd1", t, 1)[:],
+                in_=stat[("y_sum_sq", t)][:],
+                func=ACT.Abs_reciprocal_sqrt,
+                scale=1.0 / float(D * D * D),
+                bias=eps_ln[:],
+            )
+
         def centre_and_gain(t):
             centred[t] = work.tile([P, D], F32, name="centred")
             nc.vector.scalar_tensor_tensor(
                 out=centred[t][:],
                 in0=acc[t][:],
-                scalar=stat[("mean_var", t)][:, 0:1],
+                scalar=stat[("mean1", t)],
                 in1=gain[:],
                 op0=ALU.subtract,
                 op1=ALU.mult,
@@ -305,28 +338,44 @@ def tile_bdhlayer_pc_kernel(tc, xy_sparse, decoder, x, scale, running_activity, 
         first_mean_var(0)
         first_rstd(0)
         evacuate_tile(3)
-        transpose_tile(4)
-        for t in range(TILES):
+        for t in range(TILES - 2):
             if live(t + 2):
                 multiply(t + 2)
             if live(t - 2):
                 second_shift(t - 2)
                 normalise_and_store(t - 2, nc.gpsimd)
-            if live(t + 1):
+            on_vector = live(t + 1) and t + 1 not in SCALAR_STATS
+            if on_vector:
                 first_stats(t + 1)
             centre_and_gain(t)
-            if live(t + 4):
-                evacuate_tile(t + 4)
-            if live(t + 1):
+            if on_vector:
                 first_mean_var(t + 1)
                 first_rstd(t + 1)
+            if live(t + 4):
+                transpose_tile(t + 4)
+                evacuate_tile(t + 4)
+            if t + 2 in SCALAR_STATS:
+                first_sum(t + 2)
+                first_sum_of_squares(t + 2)
             if live(t + 3):
                 quantise_tile(t + 3)
-            if live(t + 5):
-                transpose_tile(t + 5)
             add_residual(t)
             second_sum_of_squares(t)
             second_rstd(t)
-        for t in (TILES - 2, TILES - 1):
+        before, last = TILES - 2, TILES - 1
+        second_shift(before - 2)
+        normalise_and_store(before - 2, nc.gpsimd)
+        first_stats(last)
+        centre_and_gain(before)
+        first_mean_var(last)
+        first_rstd(last)
+        second_shift(before - 1)
+        centre_and_gain(last)
+        for t in (before, last):
+            add_residual(t)
+            second_sum_of_squares(t)
+            second_rstd(t)
+        normalise_and_store(before - 1, nc.vector)
+        for t in (before, last):
             second_shift(t)
             normalise_and_store(t, nc.vector)

@@ -29,7 +29,7 @@ GAIN_ROWS = D // P
 RUN = 4
 DEC_COLS_VECTOR = 5 * D // 8
 
-SCALAR_STATS = ()
+SCALAR_STATS = (6, 7)
 
 EPS_LN = 1e-5
 EPS_ACTIVITY = 1e-6
@@ -87,11 +87,13 @@ def tile_bdhlayer_pc_kernel(tc, xy_sparse, decoder, x, scale, running_activity, 
             nc.sync.dma_start(out=x_sb[:], in_=x_view[:, PAIR * j : PAIR * (j + 1), :])
             x_tiles.append(x_sb)
 
-        for cols in (slice(0, DEC_COLS_VECTOR), slice(DEC_COLS_VECTOR, D)):
-            nc.sync.dma_start(out=dec_raw[:, 0, :, cols], in_=dec_view[:, 0, :, cols])
-        load_xy(0)
-        for g in range(1, PASSES):
-            nc.sync.dma_start(out=dec_raw[:, g], in_=dec_view[:, g])
+        for g in range(PASSES):
+            if g == PASSES - 1:
+                load_xy(0)
+            nc.sync.dma_start(
+                out=dec_raw[:, g].rearrange("p t d -> p (t d)"),
+                in_=dec_view[:, g].rearrange("q t d -> q (t d)"),
+            )
         for t in range(1, TILES):
             load_xy(t)
             if t >= 3 and t % PAIR == 1:
@@ -109,10 +111,12 @@ def tile_bdhlayer_pc_kernel(tc, xy_sparse, decoder, x, scale, running_activity, 
         gain_ps = psum_y.tile([P, D], F32, name="acc")
         gain = const.tile([P, D], F32)
 
-        def spread_gain():
+        def make_gain_rows():
             nc.vector.tensor_tensor(
                 out=gain_rows[0:GAIN_ROWS, :], in0=regulation[:], in1=vectors[:, 1, :], op=ALU.mult
             )
+
+        def spread_gain():
             for j in range(GAIN_ROWS):
                 nc.tensor.matmul(
                     out=gain_ps[:, P * j : P * (j + 1)],
@@ -151,12 +155,16 @@ def tile_bdhlayer_pc_kernel(tc, xy_sparse, decoder, x, scale, running_activity, 
         centred = {}
         z = {}
 
-        def transpose_tile(t):
+        def transpose_tile(t, busy=0):
             words = xy_tiles[t][:].rearrange("p h f -> p (h f)").bitcast(F32)
             banks[t] = [
                 psum_t.tile([P, 2, 2, P], F32, name="bank_a"),
-                psum_t.tile([P, 1, 2, P], F32, name="bank_b", bufs=2),
+                psum_t.tile([P, 2, 2, P], F32, name="bank_b", bufs=2),
             ]
+            for j in range(busy):
+                nc.tensor.matmul(
+                    out=banks[t][1][:, 1, 0, :], lhsT=ident[:], rhs=ident[:], start=True, stop=True
+                )
             for g in range(PASSES):
                 for u in range(2):
                     nc.tensor.transpose(
@@ -170,7 +178,7 @@ def tile_bdhlayer_pc_kernel(tc, xy_sparse, decoder, x, scale, running_activity, 
             for b, passes in enumerate((slice(0, 2), slice(2, 3))):
                 nc.scalar.copy(
                     out=grouped[t][:, passes].bitcast(F32),
-                    in_=banks[t][b][:].rearrange("p g u r -> p g r u"),
+                    in_=banks[t][b][:, : passes.stop - passes.start].rearrange("p g u r -> p g r u"),
                 )
 
         def quantise_tile(t):
@@ -258,7 +266,7 @@ def tile_bdhlayer_pc_kernel(tc, xy_sparse, decoder, x, scale, running_activity, 
             )
 
         def add_residual(t):
-            z[t] = work.tile([P, D], F32, name="z")
+            z[t] = work.tile([P, D], F32, name="z", bufs=5)
             nc.vector.scalar_tensor_tensor(
                 out=z[t][:],
                 in0=centred[t][:],
@@ -315,39 +323,42 @@ def tile_bdhlayer_pc_kernel(tc, xy_sparse, decoder, x, scale, running_activity, 
             return 0 <= t < TILES
 
         regroup_decoder(0)
-        transpose_tile(0)
+        make_gain_rows()
         spread_gain()
-        evacuate_tile(0)
         quantise_decoder(0)
         regroup_decoder(1)
-        transpose_tile(1)
-        quantise_tile(0)
-        regroup_decoder(2)
-        quantise_decoder(1)
-        evacuate_tile(1)
-        quantise_decoder(2)
         nc.scalar.copy(out=gain[:], in_=gain_ps[:])
-        multiply(0)
-        transpose_tile(2)
-        quantise_tile(1)
+        quantise_decoder(1)
+        transpose_tile(0)
+        evacuate_tile(0)
+        regroup_decoder(2)
+        quantise_tile(0)
+        quantise_decoder(2)
+        transpose_tile(1, busy=2)
+        evacuate_tile(1)
+        transpose_tile(2, busy=2)
         evacuate_tile(2)
+        multiply(0)
+        quantise_tile(1)
         multiply(1)
-        transpose_tile(3)
         first_stats(0)
         quantise_tile(2)
+        transpose_tile(3)
+        evacuate_tile(3)
         first_mean_var(0)
         first_rstd(0)
-        evacuate_tile(3)
-        for t in range(TILES - 2):
+        for t in range(TILES - 3):
             if live(t + 2):
                 multiply(t + 2)
             if live(t - 2):
                 second_shift(t - 2)
                 normalise_and_store(t - 2, nc.gpsimd)
-            on_vector = live(t + 1) and t + 1 not in SCALAR_STATS
+            on_vector = t + 1 not in SCALAR_STATS
             if on_vector:
                 first_stats(t + 1)
             centre_and_gain(t)
+            if t + 2 in SCALAR_STATS:
+                first_sum(t + 2)
             if on_vector:
                 first_mean_var(t + 1)
                 first_rstd(t + 1)
@@ -355,27 +366,32 @@ def tile_bdhlayer_pc_kernel(tc, xy_sparse, decoder, x, scale, running_activity, 
                 transpose_tile(t + 4)
                 evacuate_tile(t + 4)
             if t + 2 in SCALAR_STATS:
-                first_sum(t + 2)
                 first_sum_of_squares(t + 2)
             if live(t + 3):
                 quantise_tile(t + 3)
             add_residual(t)
             second_sum_of_squares(t)
             second_rstd(t)
-        before, last = TILES - 2, TILES - 1
-        second_shift(before - 2)
-        normalise_and_store(before - 2, nc.gpsimd)
-        first_stats(last)
-        centre_and_gain(before)
-        first_mean_var(last)
-        first_rstd(last)
-        second_shift(before - 1)
-        centre_and_gain(last)
-        for t in (before, last):
-            add_residual(t)
-            second_sum_of_squares(t)
-            second_rstd(t)
-        normalise_and_store(before - 1, nc.vector)
-        for t in (before, last):
+        a, b, c = range(TILES - 3, TILES)
+        multiply(c)
+        second_shift(a - 2)
+        normalise_and_store(a - 2, nc.gpsimd)
+        centre_and_gain(a)
+        centre_and_gain(b)
+        first_sum(c)
+        first_sum_of_squares(c)
+        second_shift(a - 1)
+        add_residual(a)
+        second_sum_of_squares(a)
+        second_rstd(a)
+        add_residual(b)
+        second_sum_of_squares(b)
+        second_rstd(b)
+        centre_and_gain(c)
+        normalise_and_store(a - 1, nc.vector)
+        add_residual(c)
+        second_sum_of_squares(c)
+        second_rstd(c)
+        for t in (a, b, c):
             second_shift(t)
             normalise_and_store(t, nc.vector)

@@ -27,7 +27,7 @@ PAIR = 2
 PAIRS = TILES // PAIR
 GAIN_ROWS = D // P
 RUN = 4
-DEC_COLS_VECTOR = 5 * D // 8
+DEC_COLS_VECTOR = 336
 
 SCALAR_STATS = (6, 7)
 
@@ -101,17 +101,18 @@ def tile_bdhlayer_pc_kernel(tc, xy_sparse, decoder, x, scale, running_activity, 
         load_x(PAIRS - 1)
 
         regulation = const.tile([GAIN_ROWS, P], F32)
-        nc.scalar.activation(
-            out=regulation[:],
-            in_=vectors[:, 0, :],
-            func=ACT.Abs_reciprocal_sqrt,
-            scale=1.0 / TARGET_ACTIVITY,
-            bias=eps_activity[0:GAIN_ROWS, :],
-        )
         gain_ps = psum_y.tile([P, D], F32, name="acc")
         gain = const.tile([P, D], F32)
 
         def make_gain_rows():
+            nc.scalar.activation(
+                out=regulation[:],
+                in_=vectors[:, 0, :],
+                func=ACT.Abs_reciprocal_sqrt,
+                scale=1.0 / TARGET_ACTIVITY,
+                bias=eps_activity[0:GAIN_ROWS, :],
+            )
+        def multiply_gain_rows():
             nc.vector.tensor_tensor(
                 out=gain_rows[0:GAIN_ROWS, :], in0=regulation[:], in1=vectors[:, 1, :], op=ALU.mult
             )
@@ -155,6 +156,11 @@ def tile_bdhlayer_pc_kernel(tc, xy_sparse, decoder, x, scale, running_activity, 
         centred = {}
         z = {}
 
+        def warm_up(n):
+            warm = psum_y.tile([P, D], F32, name="acc")
+            for j in range(n):
+                nc.tensor.matmul(out=warm[:, :P], lhsT=ident[:], rhs=ident[:], start=True, stop=True)
+
         def transpose_tile(t, busy=0):
             words = xy_tiles[t][:].rearrange("p h f -> p (h f)").bitcast(F32)
             banks[t] = [
@@ -192,10 +198,11 @@ def tile_bdhlayer_pc_kernel(tc, xy_sparse, decoder, x, scale, running_activity, 
                 )
             codes[t] = (xy_codes, xy_scales)
 
-        def multiply(t):
+        def multiply(t, passes=range(PASSES)):
             xy_codes, xy_scales = codes[t]
-            acc[t] = psum_y.tile([P, D], F32, name="acc")
-            for g in range(PASSES):
+            if passes[0] == 0:
+                acc[t] = psum_y.tile([P, D], F32, name="acc")
+            for g in passes:
                 nc.tensor.matmul_mx(
                     out=acc[t][:],
                     lhsT=xy_codes[:, g, :].bitcast(FP8X4),
@@ -308,7 +315,7 @@ def tile_bdhlayer_pc_kernel(tc, xy_sparse, decoder, x, scale, running_activity, 
             )
 
         def normalise_and_store(t, engine):
-            result = work.tile([P, D], F32, name="result")
+            result = work.tile([P, D], F32, name="result", bufs=TILES)
             engine.tensor_scalar(
                 out=result[:],
                 in0=z[t][:],
@@ -322,23 +329,26 @@ def tile_bdhlayer_pc_kernel(tc, xy_sparse, decoder, x, scale, running_activity, 
         def live(t):
             return 0 <= t < TILES
 
+        warm_up(8)
         regroup_decoder(0)
-        make_gain_rows()
-        spread_gain()
         quantise_decoder(0)
         regroup_decoder(1)
-        nc.scalar.copy(out=gain[:], in_=gain_ps[:])
+        make_gain_rows()
+        multiply_gain_rows()
         quantise_decoder(1)
         transpose_tile(0)
+        spread_gain()
         evacuate_tile(0)
         regroup_decoder(2)
         quantise_tile(0)
-        quantise_decoder(2)
-        transpose_tile(1, busy=2)
+        transpose_tile(1)
         evacuate_tile(1)
-        transpose_tile(2, busy=2)
+        nc.scalar.copy(out=gain[:], in_=gain_ps[:])
+        multiply(0, range(0, 2))
+        quantise_decoder(2)
+        transpose_tile(2)
         evacuate_tile(2)
-        multiply(0)
+        multiply(0, range(2, 3))
         quantise_tile(1)
         multiply(1)
         first_stats(0)

@@ -29,7 +29,7 @@ GAIN_ROWS = D // P
 RUN = 4
 DEC_COLS_VECTOR = 336
 
-SCALAR_STATS = (6, 7)
+SCALAR_STATS = (6,)
 
 EPS_LN = 1e-5
 EPS_ACTIVITY = 1e-6
@@ -314,17 +314,19 @@ def tile_bdhlayer_pc_kernel(tc, xy_sparse, decoder, x, scale, running_activity, 
                 op1=ALU.mult,
             )
 
-        def normalise_and_store(t, engine):
+        def normalise_and_store(t, engine, pieces=1):
             result = work.tile([P, D], F32, name="result", bufs=TILES)
-            engine.tensor_scalar(
-                out=result[:],
-                in0=z[t][:],
-                scalar1=stat[("rstd2", t)][:],
-                scalar2=stat[("shift2", t)][:],
-                op0=ALU.mult,
-                op1=ALU.add,
-            )
-            nc.sync.dma_start(out=out_view[:, t, :], in_=result[:])
+            for i in range(pieces):
+                cols = slice(i * D // pieces, (i + 1) * D // pieces)
+                engine.tensor_scalar(
+                    out=result[:, cols],
+                    in0=z[t][:, cols],
+                    scalar1=stat[("rstd2", t)][:],
+                    scalar2=stat[("shift2", t)][:],
+                    op0=ALU.mult,
+                    op1=ALU.add,
+                )
+                nc.sync.dma_start(out=out_view[:, t, cols], in_=result[:, cols])
 
         def live(t):
             return 0 <= t < TILES
@@ -387,21 +389,22 @@ def tile_bdhlayer_pc_kernel(tc, xy_sparse, decoder, x, scale, running_activity, 
         second_shift(a - 2)
         normalise_and_store(a - 2, nc.gpsimd)
         centre_and_gain(a)
-        centre_and_gain(b)
-        first_sum(c)
-        first_sum_of_squares(c)
-        second_shift(a - 1)
+        first_stats(c)
         add_residual(a)
         second_sum_of_squares(a)
+        first_mean_var(c)
+        first_rstd(c)
         second_rstd(a)
+        centre_and_gain(b)
+        second_shift(a - 1)
+        normalise_and_store(a - 1, nc.gpsimd)
+        centre_and_gain(c)
         add_residual(b)
         second_sum_of_squares(b)
         second_rstd(b)
-        centre_and_gain(c)
-        normalise_and_store(a - 1, nc.vector)
         add_residual(c)
         second_sum_of_squares(c)
         second_rstd(c)
         for t in (a, b, c):
             second_shift(t)
-            normalise_and_store(t, nc.vector)
+            normalise_and_store(t, nc.vector, pieces=2 if t == c else 1)

from contextlib import ExitStack

import concourse.mybir as mybir
from concourse.masks import make_identity

F32 = mybir.dt.float32
BF16 = mybir.dt.bfloat16
U32 = mybir.dt.uint32
U8 = mybir.dt.uint8
FP8X4 = mybir.dt.float8_e4m3fn_x4
ALU = mybir.AluOpType
ACT = mybir.ActivationFunctionType

P = 128
PACK = 4
K_PASS = P * PACK

HEADS = 6
TOKENS = 1024
FEATS = 256
D = 512
PASSES = HEADS * FEATS // K_PASS
HEADS_PER_PASS = K_PASS // FEATS
WORDS = FEATS // 2
TILES = TOKENS // P
PAIR = 2
PAIRS = TILES // PAIR
GAIN_ROWS = D // P
RUN = 4
DEC_COLS_VECTOR = 336

SCALAR_STATS = (6,)

EPS_LN = 1e-5
EPS_ACTIVITY = 1e-6
TARGET_ACTIVITY = 0.1

FLOPS = 2 * TOKENS * HEADS * FEATS * D


def tile_bdhlayer_pc_kernel(tc, xy_sparse, decoder, x, scale, running_activity, out):
    nc = tc.nc

    xy_view = xy_sparse[0].rearrange("h (p n) f -> p h n f", n=TILES)
    x_view = x[0, 0].rearrange("(p n) d -> p n d", n=TILES)
    out_view = out[0, 0].rearrange("(p n) d -> p n d", n=TILES)
    dec_view = decoder.rearrange("(g q t) d -> q g t d", g=PASSES, t=PACK)

    with ExitStack() as ctx:
        const = ctx.enter_context(tc.tile_pool(name="const", bufs=1))
        loads = ctx.enter_context(tc.tile_pool(name="loads", bufs=PAIRS))
        work = ctx.enter_context(tc.tile_pool(name="work", bufs=3))
        small = ctx.enter_context(tc.tile_pool(name="small", bufs=4))
        psum_t = ctx.enter_context(tc.psum_pool(name="psum_t", bufs=3))
        psum_y = ctx.enter_context(tc.psum_pool(name="psum_y", bufs=3))
        ctx.enter_context(tc.manual_schedule())

        eps_ln = const.tile([P, 1], F32)
        nc.vector.memset(eps_ln[:], EPS_LN)
        eps_activity = const.tile([P, 1], F32)
        nc.vector.memset(eps_activity[:], EPS_ACTIVITY / TARGET_ACTIVITY)
        gain_rows = const.tile([P, P], F32)
        nc.vector.memset(gain_rows[:], 0.0)
        ident = const.tile([P, P], F32)
        make_identity(nc, ident[:])
        vectors = const.tile([GAIN_ROWS, 2, P], BF16)
        dec_raw = const.tile([P, PASSES, PACK, D], BF16)

        nc.scalar.dma_start(
            out=vectors[:, 0, :], in_=running_activity.rearrange("(j c) -> j c", j=GAIN_ROWS)
        )
        nc.scalar.dma_start(
            out=vectors[:, 1, :], in_=scale.rearrange("(j c) -> j c", j=GAIN_ROWS)
        )
        warm_up = const.tile([P, 1], F32)
        nc.scalar.activation(out=warm_up[:], in_=eps_ln[:], func=ACT.Abs_reciprocal_sqrt)
        xy_tiles = []
        x_tiles = []

        def load_xy(t):
            xy_sb = loads.tile([P, HEADS, FEATS], BF16, name="xy_sb", bufs=TILES)
            nc.sync.dma_start(out=xy_sb[:], in_=xy_view[:, :, t, :])
            xy_tiles.append(xy_sb)

        def load_x(j):
            x_sb = loads.tile([P, PAIR, D], BF16, name="x_sb")
            nc.sync.dma_start(out=x_sb[:], in_=x_view[:, PAIR * j : PAIR * (j + 1), :])
            x_tiles.append(x_sb)

        for g in range(PASSES):
            if g == PASSES - 1:
                load_xy(0)
            nc.sync.dma_start(
                out=dec_raw[:, g].rearrange("p t d -> p (t d)"),
                in_=dec_view[:, g].rearrange("q t d -> q (t d)"),
            )
        for t in range(1, TILES):
            load_xy(t)
            if t >= 3 and t % PAIR == 1:
                load_x(t // PAIR - 1)
        load_x(PAIRS - 1)

        regulation = const.tile([GAIN_ROWS, P], F32)
        gain_ps = psum_y.tile([P, D], F32, name="acc")
        gain = const.tile([P, D], F32)

        def make_gain_rows():
            nc.scalar.activation(
                out=regulation[:],
                in_=vectors[:, 0, :],
                func=ACT.Abs_reciprocal_sqrt,
                scale=1.0 / TARGET_ACTIVITY,
                bias=eps_activity[0:GAIN_ROWS, :],
            )
        def multiply_gain_rows():
            nc.vector.tensor_tensor(
                out=gain_rows[0:GAIN_ROWS, :], in0=regulation[:], in1=vectors[:, 1, :], op=ALU.mult
            )

        def spread_gain():
            for j in range(GAIN_ROWS):
                nc.tensor.matmul(
                    out=gain_ps[:, P * j : P * (j + 1)],
                    lhsT=ident[:, j : j + 1].to_broadcast([P, P]),
                    rhs=gain_rows[:],
                    start=True,
                    stop=True,
                )

        dec_grouped = const.tile([P, PASSES, D, PACK], BF16, align_bytes=64)
        dec_codes = const.tile([P, PASSES, D], U32, align_bytes=64)
        dec_scales = const.tile([P, PASSES, D], U8, align_bytes=64)

        def regroup_decoder(g):
            nc.vector.tensor_copy(
                out=dec_grouped[:, g, :DEC_COLS_VECTOR, :].rearrange("p (c i) t -> p c t i", i=RUN),
                in_=dec_raw[:, g, :, :DEC_COLS_VECTOR].rearrange("p t (c i) -> p c t i", i=RUN),
            )
            nc.scalar.copy(
                out=dec_grouped[:, g, DEC_COLS_VECTOR:, :].rearrange("p (c i) t -> p c t i", i=RUN),
                in_=dec_raw[:, g, :, DEC_COLS_VECTOR:].rearrange("p t (c i) -> p c t i", i=RUN),
            )

        def quantise_decoder(g):
            nc.vector.quantize_mx(
                out=dec_codes[:, g, :].bitcast(FP8X4),
                scales=dec_scales[:, g, :],
                in_=dec_grouped[:, g].rearrange("p d t -> p (d t)"),
            )

        banks = {}
        grouped = {}
        codes = {}
        acc = {}
        stat = {}
        centred = {}
        z = {}

        def warm_up(n):
            warm = psum_y.tile([P, D], F32, name="acc")
            for j in range(n):
                nc.tensor.matmul(out=warm[:, :P], lhsT=ident[:], rhs=ident[:], start=True, stop=True)

        def transpose_tile(t, busy=0):
            words = xy_tiles[t][:].rearrange("p h f -> p (h f)").bitcast(F32)
            banks[t] = [
                psum_t.tile([P, 2, 2, P], F32, name="bank_a"),
                psum_t.tile([P, 2, 2, P], F32, name="bank_b", bufs=2),
            ]
            for j in range(busy):
                nc.tensor.matmul(
                    out=banks[t][1][:, 1, 0, :], lhsT=ident[:], rhs=ident[:], start=True, stop=True
                )
            for g in range(PASSES):
                for u in range(2):
                    nc.tensor.transpose(
                        banks[t][g // 2][:, g % 2, u, :],
                        words[:, 2 * P * g + u : 2 * P * (g + 1) : 2],
                        ident[:],
                    )

        def evacuate_tile(t):
            grouped[t] = work.tile([P, PASSES, P, PACK], BF16, align_bytes=64, name="xy_grouped")
            for b, passes in enumerate((slice(0, 2), slice(2, 3))):
                nc.scalar.copy(
                    out=grouped[t][:, passes].bitcast(F32),
                    in_=banks[t][b][:, : passes.stop - passes.start].rearrange("p g u r -> p g r u"),
                )

        def quantise_tile(t):
            xy_codes = work.tile([P, PASSES, P], U32, align_bytes=64, name="xy_codes")
            xy_scales = work.tile([P, PASSES, P], U8, align_bytes=64, name="xy_scales")
            for passes in (slice(0, 2), slice(2, 3)):
                nc.vector.quantize_mx(
                    out=xy_codes[:, passes, :].rearrange("p g r -> p (g r)").bitcast(FP8X4),
                    scales=xy_scales[:, passes, :].rearrange("p g r -> p (g r)"),
                    in_=grouped[t][:, passes].rearrange("p g r t -> p (g r t)"),
                )
            codes[t] = (xy_codes, xy_scales)

        def multiply(t, passes=range(PASSES)):
            xy_codes, xy_scales = codes[t]
            if passes[0] == 0:
                acc[t] = psum_y.tile([P, D], F32, name="acc")
            for g in passes:
                nc.tensor.matmul_mx(
                    out=acc[t][:],
                    lhsT=xy_codes[:, g, :].bitcast(FP8X4),
                    lhsT_scale=xy_scales[:, g, :],
                    rhs=dec_codes[:, g, :].bitcast(FP8X4),
                    rhs_scale=dec_scales[:, g, :],
                    start=(g == 0),
                    stop=(g == PASSES - 1),
                )

        def new_stat(name, t, width):
            stat[(name, t)] = small.tile([P, width], F32, name=name)
            return stat[(name, t)]

        def first_stats(t):
            nc.vector.bn_stats(out=new_stat("partial", t, 6)[:], in_=acc[t][:])

        def first_mean_var(t):
            mean_var = new_stat("mean_var", t, 2)
            nc.vector.bn_aggr(out=mean_var[:], in_=stat[("partial", t)][:])
            stat[("mean1", t)] = mean_var[:, 0:1]

        def first_rstd(t):
            nc.scalar.activation(
                out=new_stat("rstd1", t, 1)[:],
                in_=stat[("mean_var", t)][:, 1:2],
                func=ACT.Abs_reciprocal_sqrt,
                bias=eps_ln[:],
            )

        def first_sum(t):
            passed = work.tile([P, D], F32, name="passed")
            nc.scalar.activation(
                out=passed[:], in_=acc[t][:], func=ACT.Identity, accum_out=new_stat("y_sum", t, 1)[:]
            )

        def first_sum_of_squares(t):
            passed = work.tile([P, D], F32, name="passed")
            nc.scalar.activation(
                out=passed[:],
                in_=acc[t][:],
                func=ACT.Square,
                scale=-float(D),
                bias=stat[("y_sum", t)][:],
                accum_out=new_stat("y_sum_sq", t, 1)[:],
            )
            stat[("mean1", t)] = new_stat("y_mean", t, 1)[:]
            nc.scalar.activation(
                out=stat[("mean1", t)], in_=stat[("y_sum", t)][:], func=ACT.Copy, scale=1.0 / float(D)
            )
            nc.scalar.activation(
                out=new_stat("rstd1", t, 1)[:],
                in_=stat[("y_sum_sq", t)][:],
                func=ACT.Abs_reciprocal_sqrt,
                scale=1.0 / float(D * D * D),
                bias=eps_ln[:],
            )

        def centre_and_gain(t):
            centred[t] = work.tile([P, D], F32, name="centred")
            nc.vector.scalar_tensor_tensor(
                out=centred[t][:],
                in0=acc[t][:],
                scalar=stat[("mean1", t)],
                in1=gain[:],
                op0=ALU.subtract,
                op1=ALU.mult,
            )

        def add_residual(t):
            z[t] = work.tile([P, D], F32, name="z", bufs=5)
            nc.vector.scalar_tensor_tensor(
                out=z[t][:],
                in0=centred[t][:],
                scalar=stat[("rstd1", t)][:],
                in1=x_tiles[t // PAIR][:, t % PAIR, :],
                op0=ALU.mult,
                op1=ALU.add,
                accum_out=new_stat("z_sum", t, 1)[:],
            )

        def second_sum_of_squares(t):
            squares = work.tile([P, D], F32, name="squares")
            nc.scalar.activation(
                out=squares[:],
                in_=z[t][:],
                func=ACT.Square,
                scale=-float(D),
                bias=stat[("z_sum", t)][:],
                accum_out=new_stat("sum_sq", t, 1)[:],
            )

        def second_rstd(t):
            nc.scalar.activation(
                out=new_stat("rstd2", t, 1)[:],
                in_=stat[("sum_sq", t)][:],
                func=ACT.Abs_reciprocal_sqrt,
                scale=1.0 / float(D * D * D),
                bias=eps_ln[:],
            )

        def second_shift(t):
            nc.vector.tensor_scalar(
                out=new_stat("shift2", t, 1)[:],
                in0=stat[("z_sum", t)][:],
                scalar1=stat[("rstd2", t)][:],
                scalar2=-1.0 / float(D),
                op0=ALU.mult,
                op1=ALU.mult,
            )

        def normalise_and_store(t, engine, pieces=1):
            result = work.tile([P, D], F32, name="result", bufs=TILES)
            for i in range(pieces):
                cols = slice(i * D // pieces, (i + 1) * D // pieces)
                engine.tensor_scalar(
                    out=result[:, cols],
                    in0=z[t][:, cols],
                    scalar1=stat[("rstd2", t)][:],
                    scalar2=stat[("shift2", t)][:],
                    op0=ALU.mult,
                    op1=ALU.add,
                )
                nc.sync.dma_start(out=out_view[:, t, cols], in_=result[:, cols])

        def live(t):
            return 0 <= t < TILES

        warm_up(8)
        regroup_decoder(0)
        quantise_decoder(0)
        regroup_decoder(1)
        make_gain_rows()
        multiply_gain_rows()
        quantise_decoder(1)
        transpose_tile(0)
        spread_gain()
        evacuate_tile(0)
        regroup_decoder(2)
        quantise_tile(0)
        transpose_tile(1)
        evacuate_tile(1)
        nc.scalar.copy(out=gain[:], in_=gain_ps[:])
        multiply(0, range(0, 2))
        quantise_decoder(2)
        transpose_tile(2)
        evacuate_tile(2)
        multiply(0, range(2, 3))
        quantise_tile(1)
        multiply(1)
        first_stats(0)
        quantise_tile(2)
        transpose_tile(3)
        evacuate_tile(3)
        first_mean_var(0)
        first_rstd(0)
        for t in range(TILES - 3):
            if live(t + 2):
                multiply(t + 2)
            if live(t - 2):
                second_shift(t - 2)
                normalise_and_store(t - 2, nc.gpsimd)
            on_vector = t + 1 not in SCALAR_STATS
            if on_vector:
                first_stats(t + 1)
            centre_and_gain(t)
            if t + 2 in SCALAR_STATS:
                first_sum(t + 2)
            if on_vector:
                first_mean_var(t + 1)
                first_rstd(t + 1)
            if live(t + 4):
                transpose_tile(t + 4)
                evacuate_tile(t + 4)
            if t + 2 in SCALAR_STATS:
                first_sum_of_squares(t + 2)
            if live(t + 3):
                quantise_tile(t + 3)
            add_residual(t)
            second_sum_of_squares(t)
            second_rstd(t)
        a, b, c = range(TILES - 3, TILES)
        multiply(c)
        second_shift(a - 2)
        normalise_and_store(a - 2, nc.gpsimd)
        centre_and_gain(a)
        first_stats(c)
        add_residual(a)
        second_sum_of_squares(a)
        first_mean_var(c)
        first_rstd(c)
        second_rstd(a)
        centre_and_gain(b)
        second_shift(a - 1)
        normalise_and_store(a - 1, nc.gpsimd)
        centre_and_gain(c)
        add_residual(b)
        second_sum_of_squares(b)
        second_rstd(b)
        add_residual(c)
        second_sum_of_squares(c)
        second_rstd(c)
        for t in (a, b, c):
            second_shift(t)
            normalise_and_store(t, nc.vector, pieces=2 if t == c else 1)
